import numpy as np
import ml_dtypes


def mxq(x, axis, fmt="e4m3"):
    dtype, down = {"e4m3": (ml_dtypes.float8_e4m3fn, 7), "e5m2": (ml_dtypes.float8_e5m2, 14)}[fmt]
    v = np.moveaxis(np.asarray(x, np.float32).astype(ml_dtypes.bfloat16).astype(np.float64), axis, -1)
    blocks = v.reshape(v.shape[:-1] + (-1, 32))
    amax = np.abs(blocks).max(-1, keepdims=True)
    byte = np.maximum(np.where(amax > 0, np.frexp(amax)[1] - 1 + 127, 0) - down, 1)
    scale = np.exp2(byte - 127.0)
    codes = (blocks / scale).astype(np.float32).astype(dtype).astype(np.float64)
    return np.moveaxis((codes * scale).reshape(v.shape), -1, axis)


WIDE = False


def mx_kscale(k):
    if not WIDE:
        return np.ones(k)
    levels = np.array([20, -20, 10, -10, 0])
    a = np.random.permutation(np.resize(levels, k // 512 * 4)).reshape(k // 512, 4)
    idx = np.arange(k)
    return np.exp2(a[idx // 512, idx % 128 // 32])


BF16 = ml_dtypes.bfloat16


def bf(x):
    return np.asarray(x, np.float32).astype(BF16)


def f64(x):
    return np.asarray(x).astype(np.float64)


B, HH, WW, C, NH, KD, WS, SS = 2, 16, 16, 8192, 8, 64, 8, 4
GH, GW, T, F = HH // WS, WW // WS, WS * WS, NH * KD
N = B * GH * GW


def setup_inputs():
    u = mx_kscale(C)
    attn_ctx = np.random.standard_normal((N, T, NH, KD)) * 0.4
    x = np.random.standard_normal((B, HH, WW, C))
    wo = np.random.standard_normal((NH, KD, C)) * 2.0 / np.sqrt(F) / u
    bo = np.random.standard_normal(C) * 0.3
    g = np.random.standard_normal((B, HH, WW, C)) * np.exp2(np.random.randint(-12, 1, (B, HH, WW, 1))) * 4.0 * u
    return {"attn_ctx": bf(attn_ctx), "x": bf(x), "wo": bf(wo), "bo": bf(bo), "grad_out": bf(g)}


def reference(attn_ctx, x, wo, bo, grad_out):
    g = np.roll(f64(grad_out), shift=(-SS, -SS), axis=(1, 2))
    g = g.reshape(B, GH, WS, GW, WS, C).swapaxes(2, 3).reshape(N * T, C)
    go = mxq(g, 1, "e5m2") @ mxq(f64(wo).reshape(F, C), 1, "e4m3").T
    return go.reshape(N, T, NH, KD)

@@ -1,0 +1,147 @@
+from contextlib import ExitStack
+
+import concourse.mybir as mybir
+from concourse.masks import make_identity
+
+F32 = mybir.dt.float32
+BF16 = mybir.dt.bfloat16
+U32 = mybir.dt.uint32
+U8 = mybir.dt.uint8
+E5M2_X4 = mybir.dt.float8_e5m2_x4
+E4M3_X4 = mybir.dt.float8_e4m3fn_x4
+
+P = 128
+CHANNELS = 8192
+ROWS = 512
+ROW_TILES = ROWS // P
+K_PASS = 512
+PASSES = CHANNELS // K_PASS
+WORDS_PASS = K_PASS // 2
+HALVES = WORDS_PASS // P
+BANK_TILES = 2
+BANK_ROWS = BANK_TILES * P
+LOAD_PASSES = 2
+LOADS = PASSES // LOAD_PASSES
+LOAD_K = LOAD_PASSES * K_PASS
+
+FLOPS = 2 * ROWS * ROWS * CHANNELS
+BYTES = 2 * ROWS * CHANNELS * 2 + ROWS * ROWS * 4
+
+
+def window_columns(nc, matrix, ident):
+    nc.vector.tensor_copy(out=matrix[:, 0, :, :], in_=ident[:, :, 4:12])
+    nc.vector.tensor_copy(out=matrix[:, 1, :, 0:4], in_=ident[:, :, 12:16])
+    nc.vector.tensor_copy(out=matrix[:, 1, :, 4:8], in_=ident[:, :, 0:4])
+
+
+def tile_windowattentionblock_pb_k_kernel(tc, attn_ctx, x, wo, bo, grad_out, out):
+    nc = tc.nc
+    pixels = grad_out.rearrange("b i j c -> b (i j) c")
+    wo_rows = wo.rearrange("h d c -> (h d) c").rearrange("(t p) c -> p t c", p=P)
+    out_rows = out.rearrange("n t h d -> (n t) (h d)")
+
+    with ExitStack() as ctx:
+        ctx.enter_context(tc.manual_schedule())
+        consts = ctx.enter_context(tc.tile_pool(name="consts", bufs=1))
+        raw = ctx.enter_context(tc.tile_pool(name="raw", bufs=LOADS))
+        stage = ctx.enter_context(tc.tile_pool(name="stage", bufs=3))
+        results = ctx.enter_context(tc.tile_pool(name="results", bufs=ROW_TILES))
+        turn_psum = ctx.enter_context(tc.psum_pool(name="turn_psum", bufs=4))
+        acc_psum = ctx.enter_context(tc.psum_pool(name="acc_psum", bufs=1))
+
+        g_loaded = []
+        wo_loaded = []
+        for s in range(LOADS):
+            k_cols = slice(s * LOAD_K, (s + 1) * LOAD_K)
+            g_raw = raw.tile([P, ROW_TILES, LOAD_K], BF16)
+            g_by_gi = g_raw[:].rearrange("p (b gi) k -> p gi b k", gi=2)
+            nc.sync.dma_start(out=g_by_gi[:, 0], in_=pixels[:, 64:192, k_cols].rearrange("b p k -> p b k"))
+            nc.sync.dma_start(out=g_by_gi[0:P:2, 1], in_=pixels[:, 192:256, k_cols].rearrange("b p k -> p b k"))
+            nc.sync.dma_start(out=g_by_gi[1:P:2, 1], in_=pixels[:, 0:64, k_cols].rearrange("b p k -> p b k"))
+            wo_raw = raw.tile([P, ROW_TILES, LOAD_K], BF16)
+            nc.sync.dma_start(out=wo_raw[:], in_=wo_rows[:, :, k_cols])
+            g_loaded.append(g_raw)
+            wo_loaded.append(wo_raw)
+
+        ident = consts.tile([P, P], F32)
+        make_identity(nc, ident[:])
+        order_gi0 = consts.tile([P, P], F32)
+        window_columns(
+            nc,
+            order_gi0[:].rearrange("p (gj ti tj) -> p gj ti tj", gj=2, ti=8),
+            ident[:].rearrange("p (ti j) -> p ti j", j=16),
+        )
+        order_gi1 = consts.tile([P, P], F32)
+        for th in range(2):
+            window_columns(
+                nc,
+                order_gi1[:].rearrange("p (gj th i4 tj) -> p gj th i4 tj", gj=2, th=2, i4=4)[:, :, th],
+                ident[:].rearrange("p (i4 j th) -> p th i4 j", j=16, th=2)[:, th],
+            )
+        g_order = [order_gi0, order_gi1, order_gi0, order_gi1]
+        wo_order = [ident] * ROW_TILES
+
+        acc = [acc_psum.tile([P, ROWS], F32, name="acc%d" % m) for m in range(ROW_TILES)]
+
+        def turn(loaded, order, c):
+            words = loaded[c // LOAD_PASSES][:].bitcast(F32)
+            first = (c % LOAD_PASSES) * WORDS_PASS
+            banks = []
+            for pair in range(ROW_TILES // BANK_TILES):
+                turned = turn_psum.tile([P, HALVES, BANK_ROWS], F32)
+                for i in range(BANK_TILES):
+                    m = pair * BANK_TILES + i
+                    for u in range(HALVES):
+                        nc.tensor.transpose(
+                            out=turned[:, u, i * P : (i + 1) * P],
+                            in_=words[:, m, first + u * P : first + (u + 1) * P],
+                            identity=order[m][:],
+                        )
+                banks.append(turned)
+            return banks
+
+        def group(copies, banks, grouped):
+            pairs = grouped[:].bitcast(F32).rearrange("p (r u) -> p r u", u=HALVES)
+            for copy, turned, pair in zip(copies, banks, range(len(banks))):
+                copy(
+                    out=pairs[:, pair * BANK_ROWS : (pair + 1) * BANK_ROWS, :],
+                    in_=turned[:].rearrange("p u r -> p r u"),
+                )
+
+        quantised = {}
+        for c in range(PASSES + 1):
+            if c < PASSES:
+                g_banks = turn(g_loaded, g_order, c)
+                wo_banks = turn(wo_loaded, wo_order, c)
+
+            if c > 0:
+                g_codes, g_scales, wo_codes, wo_scales = quantised[c - 1]
+                for m in range(ROW_TILES):
+                    nc.tensor.matmul_mx(
+                        out=acc[m][:],
+                        lhsT=g_codes[:, m * P : (m + 1) * P].bitcast(E5M2_X4),
+                        lhsT_scale=g_scales[:, m * P : (m + 1) * P],
+                        rhs=wo_codes[:].bitcast(E4M3_X4),
+                        rhs_scale=wo_scales[:],
+                        start=(c - 1 == 0),
+                        stop=(c - 1 == PASSES - 1),
+                    )
+
+            if c < PASSES:
+                g_grouped = stage.tile([P, ROWS * 4], BF16, align_bytes=64)
+                wo_grouped = stage.tile([P, ROWS * 4], BF16, align_bytes=64)
+                group([nc.vector.tensor_copy, nc.scalar.copy], g_banks, g_grouped)
+                group([nc.scalar.copy, nc.scalar.copy], wo_banks, wo_grouped)
+                g_codes = stage.tile([P, ROWS], U32, align_bytes=64)
+                g_scales = stage.tile([P, ROWS], U8, align_bytes=64)
+                nc.vector.quantize_mx(out=g_codes[:].bitcast(E5M2_X4), scales=g_scales[:], in_=g_grouped[:])
+                wo_codes = stage.tile([P, ROWS], U32, align_bytes=64)
+                wo_scales = stage.tile([P, ROWS], U8, align_bytes=64)
+                nc.vector.quantize_mx(out=wo_codes[:].bitcast(E4M3_X4), scales=wo_scales[:], in_=wo_grouped[:])
+                quantised[c] = (g_codes, g_scales, wo_codes, wo_scales)
+
+        for m in range(ROW_TILES):
+            result = results.tile([P, ROWS], F32)
+            copy = nc.scalar.copy if m % 2 == 0 else nc.vector.tensor_copy
+            copy(out=result[:], in_=acc[m][:])
+            nc.sync.dma_start(out=out_rows[m * P : (m + 1) * P, :], in_=result[:])

@@ -108,24 +108,29 @@ def tile_windowattentionblock_pb_k_kernel(tc, attn_ctx, x, wo, bo, grad_out, out
                     in_=turned[:].rearrange("p u r -> p r u"),
                 )
 
+        def multiply(c, row_tiles):
+            g_codes, g_scales, wo_codes, wo_scales = quantised[c]
+            for m in row_tiles:
+                nc.tensor.matmul_mx(
+                    out=acc[m][:],
+                    lhsT=g_codes[:, m * P : (m + 1) * P].bitcast(E5M2_X4),
+                    lhsT_scale=g_scales[:, m * P : (m + 1) * P],
+                    rhs=wo_codes[:].bitcast(E4M3_X4),
+                    rhs_scale=wo_scales[:],
+                    start=(c == 0),
+                    stop=(c == PASSES - 1),
+                )
+
         quantised = {}
-        for c in range(PASSES + 1):
+        for c in range(PASSES + 2):
             if c < PASSES:
                 g_banks = turn(g_loaded, g_order, c)
+            if 0 <= c - 2:
+                multiply(c - 2, [2, 3])
+            if c < PASSES:
                 wo_banks = turn(wo_loaded, wo_order, c)
-
-            if c > 0:
-                g_codes, g_scales, wo_codes, wo_scales = quantised[c - 1]
-                for m in range(ROW_TILES):
-                    nc.tensor.matmul_mx(
-                        out=acc[m][:],
-                        lhsT=g_codes[:, m * P : (m + 1) * P].bitcast(E5M2_X4),
-                        lhsT_scale=g_scales[:, m * P : (m + 1) * P],
-                        rhs=wo_codes[:].bitcast(E4M3_X4),
-                        rhs_scale=wo_scales[:],
-                        start=(c - 1 == 0),
-                        stop=(c - 1 == PASSES - 1),
-                    )
+            if 0 <= c - 1 < PASSES:
+                multiply(c - 1, [0, 1])
 
             if c < PASSES:
                 g_grouped = stage.tile([P, ROWS * 4], BF16, align_bytes=64)

@@ -20,6 +20,9 @@ WORDS_PASS = K_PASS // 2
 HALVES = WORDS_PASS // P
 BANK_TILES = 2
 BANK_ROWS = BANK_TILES * P
+PASS_BANKS = 2 * ROW_TILES // BANK_TILES
+RUN = 3
+LAG = 2
 LOAD_PASSES = 2
 LOADS = PASSES // LOAD_PASSES
 LOAD_K = LOAD_PASSES * K_PASS
@@ -83,67 +86,72 @@ def tile_windowattentionblock_pb_k_kernel(tc, attn_ctx, x, wo, bo, grad_out, out
 
         acc = [acc_psum.tile([P, ROWS], F32, name="acc%d" % m) for m in range(ROW_TILES)]
 
-        def turn(loaded, order, c):
+        def turn(loaded, order, c, pair):
             words = loaded[c // LOAD_PASSES][:].bitcast(F32)
             first = (c % LOAD_PASSES) * WORDS_PASS
-            banks = []
-            for pair in range(ROW_TILES // BANK_TILES):
-                turned = turn_psum.tile([P, HALVES, BANK_ROWS], F32)
-                for i in range(BANK_TILES):
-                    m = pair * BANK_TILES + i
-                    for u in range(HALVES):
-                        nc.tensor.transpose(
-                            out=turned[:, u, i * P : (i + 1) * P],
-                            in_=words[:, m, first + u * P : first + (u + 1) * P],
-                            identity=order[m][:],
-                        )
-                banks.append(turned)
-            return banks
+            turned = turn_psum.tile([P, HALVES, BANK_ROWS], F32)
+            for i in range(BANK_TILES):
+                m = pair * BANK_TILES + i
+                for u in range(HALVES):
+                    nc.tensor.transpose(
+                        out=turned[:, u, i * P : (i + 1) * P],
+                        in_=words[:, m, first + u * P : first + (u + 1) * P],
+                        identity=order[m][:],
+                    )
+            return turned
 
-        def group(copies, banks, grouped):
+        def group(copy, turned, grouped, pair):
             pairs = grouped[:].bitcast(F32).rearrange("p (r u) -> p r u", u=HALVES)
-            for copy, turned, pair in zip(copies, banks, range(len(banks))):
-                copy(
-                    out=pairs[:, pair * BANK_ROWS : (pair + 1) * BANK_ROWS, :],
-                    in_=turned[:].rearrange("p u r -> p r u"),
-                )
-
-        def multiply(c, row_tiles):
-            g_codes, g_scales, wo_codes, wo_scales = quantised[c]
-            for m in row_tiles:
-                nc.tensor.matmul_mx(
-                    out=acc[m][:],
-                    lhsT=g_codes[:, m * P : (m + 1) * P].bitcast(E5M2_X4),
-                    lhsT_scale=g_scales[:, m * P : (m + 1) * P],
-                    rhs=wo_codes[:].bitcast(E4M3_X4),
-                    rhs_scale=wo_scales[:],
-                    start=(c == 0),
-                    stop=(c == PASSES - 1),
-                )
+            copy(
+                out=pairs[:, pair * BANK_ROWS : (pair + 1) * BANK_ROWS, :],
+                in_=turned[:].rearrange("p u r -> p r u"),
+            )
 
         quantised = {}
-        for c in range(PASSES + 2):
-            if c < PASSES:
-                g_banks = turn(g_loaded, g_order, c)
-            if 0 <= c - 2:
-                multiply(c - 2, [2, 3])
-            if c < PASSES:
-                wo_banks = turn(wo_loaded, wo_order, c)
-            if 0 <= c - 1 < PASSES:
-                multiply(c - 1, [0, 1])
 
-            if c < PASSES:
-                g_grouped = stage.tile([P, ROWS * 4], BF16, align_bytes=64)
-                wo_grouped = stage.tile([P, ROWS * 4], BF16, align_bytes=64)
-                group([nc.vector.tensor_copy, nc.scalar.copy], g_banks, g_grouped)
-                group([nc.scalar.copy, nc.scalar.copy], wo_banks, wo_grouped)
-                g_codes = stage.tile([P, ROWS], U32, align_bytes=64)
-                g_scales = stage.tile([P, ROWS], U8, align_bytes=64)
+        def prepare(bank):
+            c, i = divmod(bank, PASS_BANKS)
+            if i == 0:
+                g_grouped = stage.tile([P, ROWS * 4], BF16, align_bytes=64, name="g_grouped")
+                wo_grouped = stage.tile([P, ROWS * 4], BF16, align_bytes=64, name="wo_grouped")
+                quantised[c] = [g_grouped, wo_grouped]
+            g_grouped, wo_grouped = quantised[c][0:2]
+            if i == 0:
+                group(nc.vector.tensor_copy, turn(g_loaded, g_order, c, 0), g_grouped, 0)
+            if i == 1:
+                group(nc.scalar.copy, turn(g_loaded, g_order, c, 1), g_grouped, 1)
+                g_codes = stage.tile([P, ROWS], U32, align_bytes=64, name="g_codes")
+                g_scales = stage.tile([P, ROWS], U8, align_bytes=64, name="g_scales")
                 nc.vector.quantize_mx(out=g_codes[:].bitcast(E5M2_X4), scales=g_scales[:], in_=g_grouped[:])
-                wo_codes = stage.tile([P, ROWS], U32, align_bytes=64)
-                wo_scales = stage.tile([P, ROWS], U8, align_bytes=64)
+                quantised[c].extend([g_codes, g_scales])
+            if i == 2:
+                group(nc.scalar.copy, turn(wo_loaded, wo_order, c, 0), wo_grouped, 0)
+            if i == 3:
+                group(nc.scalar.copy, turn(wo_loaded, wo_order, c, 1), wo_grouped, 1)
+                wo_codes = stage.tile([P, ROWS], U32, align_bytes=64, name="wo_codes")
+                wo_scales = stage.tile([P, ROWS], U8, align_bytes=64, name="wo_scales")
                 nc.vector.quantize_mx(out=wo_codes[:].bitcast(E4M3_X4), scales=wo_scales[:], in_=wo_grouped[:])
-                quantised[c] = (g_codes, g_scales, wo_codes, wo_scales)
+                quantised[c].extend([wo_codes, wo_scales])
+
+        def multiply(product):
+            c, m = divmod(product, ROW_TILES)
+            g_codes, g_scales, wo_codes, wo_scales = quantised[c][2:6]
+            nc.tensor.matmul_mx(
+                out=acc[m][:],
+                lhsT=g_codes[:, m * P : (m + 1) * P].bitcast(E5M2_X4),
+                lhsT_scale=g_scales[:, m * P : (m + 1) * P],
+                rhs=wo_codes[:].bitcast(E4M3_X4),
+                rhs_scale=wo_scales[:],
+                start=(c == 0),
+                stop=(c == PASSES - 1),
+            )
+
+        rounds = -(-PASSES * PASS_BANKS // RUN) + LAG
+        for r in range(rounds):
+            for bank in range(r * RUN, min((r + 1) * RUN, PASSES * PASS_BANKS)):
+                prepare(bank)
+            for product in range(max((r - LAG) * RUN, 0), min((r - LAG + 1) * RUN, PASSES * ROW_TILES)):
+                multiply(product)
 
         for m in range(ROW_TILES):
             result = results.tile([P, ROWS], F32)

@@ -21,7 +21,7 @@ HALVES = WORDS_PASS // P
 BANK_TILES = 2
 BANK_ROWS = BANK_TILES * P
 PASS_BANKS = 2 * ROW_TILES // BANK_TILES
-RUN = 3
+RUN = 4
 LAG = 2
 LOAD_PASSES = 2
 LOADS = PASSES // LOAD_PASSES
@@ -47,7 +47,7 @@ def tile_windowattentionblock_pb_k_kernel(tc, attn_ctx, x, wo, bo, grad_out, out
         ctx.enter_context(tc.manual_schedule())
         consts = ctx.enter_context(tc.tile_pool(name="consts", bufs=1))
         raw = ctx.enter_context(tc.tile_pool(name="raw", bufs=LOADS))
-        stage = ctx.enter_context(tc.tile_pool(name="stage", bufs=3))
+        stage = ctx.enter_context(tc.tile_pool(name="stage", bufs=4))
         results = ctx.enter_context(tc.tile_pool(name="results", bufs=ROW_TILES))
         turn_psum = ctx.enter_context(tc.psum_pool(name="turn_psum", bufs=4))
         acc_psum = ctx.enter_context(tc.psum_pool(name="acc_psum", bufs=1))

@@ -20,12 +20,11 @@ WORDS_PASS = K_PASS // 2
 HALVES = WORDS_PASS // P
 BANK_TILES = 2
 BANK_ROWS = BANK_TILES * P
-PASS_BANKS = 2 * ROW_TILES // BANK_TILES
-RUN = 4
-LAG = 2
+PAIRS = ROW_TILES // BANK_TILES
 LOAD_PASSES = 2
 LOADS = PASSES // LOAD_PASSES
 LOAD_K = LOAD_PASSES * K_PASS
+LAG = 3
 
 FLOPS = 2 * ROWS * ROWS * CHANNELS
 BYTES = 2 * ROWS * CHANNELS * 2 + ROWS * ROWS * 4
@@ -48,6 +47,7 @@ def tile_windowattentionblock_pb_k_kernel(tc, attn_ctx, x, wo, bo, grad_out, out
         consts = ctx.enter_context(tc.tile_pool(name="consts", bufs=1))
         raw = ctx.enter_context(tc.tile_pool(name="raw", bufs=LOADS))
         stage = ctx.enter_context(tc.tile_pool(name="stage", bufs=4))
+        operands = ctx.enter_context(tc.tile_pool(name="operands", bufs=6))
         results = ctx.enter_context(tc.tile_pool(name="results", bufs=ROW_TILES))
         turn_psum = ctx.enter_context(tc.psum_pool(name="turn_psum", bufs=4))
         acc_psum = ctx.enter_context(tc.psum_pool(name="acc_psum", bufs=1))
@@ -56,15 +56,17 @@ def tile_windowattentionblock_pb_k_kernel(tc, attn_ctx, x, wo, bo, grad_out, out
         wo_loaded = []
         for s in range(LOADS):
             k_cols = slice(s * LOAD_K, (s + 1) * LOAD_K)
-            g_raw = raw.tile([P, ROW_TILES, LOAD_K], BF16)
-            g_by_gi = g_raw[:].rearrange("p (b gi) k -> p gi b k", gi=2)
-            nc.sync.dma_start(out=g_by_gi[:, 0], in_=pixels[:, 64:192, k_cols].rearrange("b p k -> p b k"))
-            nc.sync.dma_start(out=g_by_gi[0:P:2, 1], in_=pixels[:, 192:256, k_cols].rearrange("b p k -> p b k"))
-            nc.sync.dma_start(out=g_by_gi[1:P:2, 1], in_=pixels[:, 0:64, k_cols].rearrange("b p k -> p b k"))
-            wo_raw = raw.tile([P, ROW_TILES, LOAD_K], BF16)
-            nc.sync.dma_start(out=wo_raw[:], in_=wo_rows[:, :, k_cols])
-            g_loaded.append(g_raw)
-            wo_loaded.append(wo_raw)
+            g_raw0 = raw.tile([P, BANK_TILES, LOAD_K], BF16)
+            nc.sync.dma_start(out=g_raw0[:], in_=pixels[:, 64:192, k_cols].rearrange("b p k -> p b k"))
+            g_raw1 = raw.tile([P, BANK_TILES, LOAD_K], BF16)
+            nc.sync.dma_start(out=g_raw1[0:P:2], in_=pixels[:, 192:256, k_cols].rearrange("b p k -> p b k"))
+            nc.sync.dma_start(out=g_raw1[1:P:2], in_=pixels[:, 0:64, k_cols].rearrange("b p k -> p b k"))
+            wo_raw0 = raw.tile([P, BANK_TILES, LOAD_K], BF16)
+            nc.sync.dma_start(out=wo_raw0[:], in_=wo_rows[:, 0:BANK_TILES, k_cols])
+            wo_raw1 = raw.tile([P, BANK_TILES, LOAD_K], BF16)
+            nc.sync.dma_start(out=wo_raw1[:], in_=wo_rows[:, BANK_TILES:ROW_TILES, k_cols])
+            g_loaded.append([g_raw0, g_raw1])
+            wo_loaded.append([wo_raw0, wo_raw1])
 
         ident = consts.tile([P, P], F32)
         make_identity(nc, ident[:])
@@ -81,22 +83,21 @@ def tile_windowattentionblock_pb_k_kernel(tc, attn_ctx, x, wo, bo, grad_out, out
                 order_gi1[:].rearrange("p (gj th i4 tj) -> p gj th i4 tj", gj=2, th=2, i4=4)[:, :, th],
                 ident[:].rearrange("p (i4 j th) -> p th i4 j", j=16, th=2)[:, th],
             )
-        g_order = [order_gi0, order_gi1, order_gi0, order_gi1]
-        wo_order = [ident] * ROW_TILES
+        g_order = [order_gi0, order_gi1]
+        wo_order = [ident, ident]
 
         acc = [acc_psum.tile([P, ROWS], F32, name="acc%d" % m) for m in range(ROW_TILES)]
 
         def turn(loaded, order, c, pair):
-            words = loaded[c // LOAD_PASSES][:].bitcast(F32)
+            words = loaded[c // LOAD_PASSES][pair][:].bitcast(F32)
             first = (c % LOAD_PASSES) * WORDS_PASS
             turned = turn_psum.tile([P, HALVES, BANK_ROWS], F32)
             for i in range(BANK_TILES):
-                m = pair * BANK_TILES + i
                 for u in range(HALVES):
                     nc.tensor.transpose(
                         out=turned[:, u, i * P : (i + 1) * P],
-                        in_=words[:, m, first + u * P : first + (u + 1) * P],
-                        identity=order[m][:],
+                        in_=words[:, i, first + u * P : first + (u + 1) * P],
+                        identity=order[pair][:],
                     )
             return turned
 
@@ -107,51 +108,49 @@ def tile_windowattentionblock_pb_k_kernel(tc, attn_ctx, x, wo, bo, grad_out, out
                 in_=turned[:].rearrange("p u r -> p r u"),
             )
 
-        quantised = {}
+        g_quantised = {}
+        wo_quantised = {}
 
-        def prepare(bank):
-            c, i = divmod(bank, PASS_BANKS)
-            if i == 0:
-                g_grouped = stage.tile([P, ROWS * 4], BF16, align_bytes=64, name="g_grouped")
-                wo_grouped = stage.tile([P, ROWS * 4], BF16, align_bytes=64, name="wo_grouped")
-                quantised[c] = [g_grouped, wo_grouped]
-            g_grouped, wo_grouped = quantised[c][0:2]
-            if i == 0:
-                group(nc.vector.tensor_copy, turn(g_loaded, g_order, c, 0), g_grouped, 0)
-            if i == 1:
-                group(nc.scalar.copy, turn(g_loaded, g_order, c, 1), g_grouped, 1)
-                g_codes = stage.tile([P, ROWS], U32, align_bytes=64, name="g_codes")
-                g_scales = stage.tile([P, ROWS], U8, align_bytes=64, name="g_scales")
-                nc.vector.quantize_mx(out=g_codes[:].bitcast(E5M2_X4), scales=g_scales[:], in_=g_grouped[:])
-                quantised[c].extend([g_codes, g_scales])
-            if i == 2:
-                group(nc.scalar.copy, turn(wo_loaded, wo_order, c, 0), wo_grouped, 0)
-            if i == 3:
-                group(nc.scalar.copy, turn(wo_loaded, wo_order, c, 1), wo_grouped, 1)
-                wo_codes = stage.tile([P, ROWS], U32, align_bytes=64, name="wo_codes")
-                wo_scales = stage.tile([P, ROWS], U8, align_bytes=64, name="wo_scales")
-                nc.vector.quantize_mx(out=wo_codes[:].bitcast(E4M3_X4), scales=wo_scales[:], in_=wo_grouped[:])
-                quantised[c].extend([wo_codes, wo_scales])
+        def prepare(name, loaded, order, x4, quantised, first_pass):
+            passes = range(first_pass, first_pass + LOAD_PASSES)
+            grouped = {}
+            for c in passes:
+                grouped[c] = stage.tile([P, ROWS * 4], BF16, align_bytes=64, name="grouped")
+            for pair in range(PAIRS):
+                for c in passes:
+                    copy = nc.vector.tensor_copy if (pair == 0 and c == first_pass) else nc.scalar.copy
+                    group(copy, turn(loaded, order, c, pair), grouped[c], pair)
+                    if pair == PAIRS - 1:
+                        codes = operands.tile([P, ROWS], U32, align_bytes=64, name=name + "_codes")
+                        scales = operands.tile([P, ROWS], U8, align_bytes=64, name=name + "_scales")
+                        nc.vector.quantize_mx(out=codes[:].bitcast(x4), scales=scales[:], in_=grouped[c][:])
+                        quantised[c] = (codes, scales)
 
-        def multiply(product):
-            c, m = divmod(product, ROW_TILES)
-            g_codes, g_scales, wo_codes, wo_scales = quantised[c][2:6]
-            nc.tensor.matmul_mx(
-                out=acc[m][:],
-                lhsT=g_codes[:, m * P : (m + 1) * P].bitcast(E5M2_X4),
-                lhsT_scale=g_scales[:, m * P : (m + 1) * P],
-                rhs=wo_codes[:].bitcast(E4M3_X4),
-                rhs_scale=wo_scales[:],
-                start=(c == 0),
-                stop=(c == PASSES - 1),
-            )
+        def multiply(c):
+            g_codes, g_scales = g_quantised[c]
+            wo_codes, wo_scales = wo_quantised[c]
+            for m in range(ROW_TILES):
+                b, gi = divmod(m, 2)
+                g_cols = slice((2 * gi + b) * P, (2 * gi + b + 1) * P)
+                nc.tensor.matmul_mx(
+                    out=acc[m][:],
+                    lhsT=g_codes[:, g_cols].bitcast(E5M2_X4),
+                    lhsT_scale=g_scales[:, g_cols],
+                    rhs=wo_codes[:].bitcast(E4M3_X4),
+                    rhs_scale=wo_scales[:],
+                    start=(c == 0),
+                    stop=(c == PASSES - 1),
+                )
 
-        rounds = -(-PASSES * PASS_BANKS // RUN) + LAG
-        for r in range(rounds):
-            for bank in range(r * RUN, min((r + 1) * RUN, PASSES * PASS_BANKS)):
-                prepare(bank)
-            for product in range(max((r - LAG) * RUN, 0), min((r - LAG + 1) * RUN, PASSES * ROW_TILES)):
-                multiply(product)
+        for k in range(PASSES + LAG):
+            if k < PASSES:
+                first_pass = k // 2 * LOAD_PASSES
+                if k % 2 == 0:
+                    prepare("g", g_loaded, g_order, E5M2_X4, g_quantised, first_pass)
+                else:
+                    prepare("wo", wo_loaded, wo_order, E4M3_X4, wo_quantised, first_pass)
+            if k >= LAG:
+                multiply(k - LAG)
 
         for m in range(ROW_TILES):
             result = results.tile([P, ROWS], F32)

@@ -24,7 +24,8 @@ PAIRS = ROW_TILES // BANK_TILES
 LOAD_PASSES = 2
 LOADS = PASSES // LOAD_PASSES
 LOAD_K = LOAD_PASSES * K_PASS
-LAG = 3
+CHUNKS = LOADS * 2 * PAIRS
+QUADS = LOADS * PAIRS
 
 FLOPS = 2 * ROWS * ROWS * CHANNELS
 BYTES = 2 * ROWS * CHANNELS * 2 + ROWS * ROWS * 4
@@ -46,8 +47,10 @@ def tile_windowattentionblock_pb_k_kernel(tc, attn_ctx, x, wo, bo, grad_out, out
         ctx.enter_context(tc.manual_schedule())
         consts = ctx.enter_context(tc.tile_pool(name="consts", bufs=1))
         raw = ctx.enter_context(tc.tile_pool(name="raw", bufs=LOADS))
-        stage = ctx.enter_context(tc.tile_pool(name="stage", bufs=4))
-        operands = ctx.enter_context(tc.tile_pool(name="operands", bufs=6))
+        wo_stage = ctx.enter_context(tc.tile_pool(name="wo_stage", bufs=4))
+        g_stage = ctx.enter_context(tc.tile_pool(name="g_stage", bufs=6))
+        wo_operands = ctx.enter_context(tc.tile_pool(name="wo_operands", bufs=6))
+        g_operands = ctx.enter_context(tc.tile_pool(name="g_operands", bufs=12))
         results = ctx.enter_context(tc.tile_pool(name="results", bufs=ROW_TILES))
         turn_psum = ctx.enter_context(tc.psum_pool(name="turn_psum", bufs=4))
         acc_psum = ctx.enter_context(tc.psum_pool(name="acc_psum", bufs=1))
@@ -56,15 +59,15 @@ def tile_windowattentionblock_pb_k_kernel(tc, attn_ctx, x, wo, bo, grad_out, out
         wo_loaded = []
         for s in range(LOADS):
             k_cols = slice(s * LOAD_K, (s + 1) * LOAD_K)
+            wo_raw0 = raw.tile([P, BANK_TILES, LOAD_K], BF16)
+            nc.sync.dma_start(out=wo_raw0[:], in_=wo_rows[:, 0:BANK_TILES, k_cols])
+            wo_raw1 = raw.tile([P, BANK_TILES, LOAD_K], BF16)
+            nc.sync.dma_start(out=wo_raw1[:], in_=wo_rows[:, BANK_TILES:ROW_TILES, k_cols])
             g_raw0 = raw.tile([P, BANK_TILES, LOAD_K], BF16)
             nc.sync.dma_start(out=g_raw0[:], in_=pixels[:, 64:192, k_cols].rearrange("b p k -> p b k"))
             g_raw1 = raw.tile([P, BANK_TILES, LOAD_K], BF16)
             nc.sync.dma_start(out=g_raw1[0:P:2], in_=pixels[:, 192:256, k_cols].rearrange("b p k -> p b k"))
             nc.sync.dma_start(out=g_raw1[1:P:2], in_=pixels[:, 0:64, k_cols].rearrange("b p k -> p b k"))
-            wo_raw0 = raw.tile([P, BANK_TILES, LOAD_K], BF16)
-            nc.sync.dma_start(out=wo_raw0[:], in_=wo_rows[:, 0:BANK_TILES, k_cols])
-            wo_raw1 = raw.tile([P, BANK_TILES, LOAD_K], BF16)
-            nc.sync.dma_start(out=wo_raw1[:], in_=wo_rows[:, BANK_TILES:ROW_TILES, k_cols])
             g_loaded.append([g_raw0, g_raw1])
             wo_loaded.append([wo_raw0, wo_raw1])
 
@@ -84,12 +87,11 @@ def tile_windowattentionblock_pb_k_kernel(tc, attn_ctx, x, wo, bo, grad_out, out
                 ident[:].rearrange("p (i4 j th) -> p th i4 j", j=16, th=2)[:, th],
             )
         g_order = [order_gi0, order_gi1]
-        wo_order = [ident, ident]
 
         acc = [acc_psum.tile([P, ROWS], F32, name="acc%d" % m) for m in range(ROW_TILES)]
 
-        def turn(loaded, order, c, pair):
-            words = loaded[c // LOAD_PASSES][pair][:].bitcast(F32)
+        def turn(raw_tile, order, c):
+            words = raw_tile[:].bitcast(F32)
             first = (c % LOAD_PASSES) * WORDS_PASS
             turned = turn_psum.tile([P, HALVES, BANK_ROWS], F32)
             for i in range(BANK_TILES):
@@ -97,63 +99,76 @@ def tile_windowattentionblock_pb_k_kernel(tc, attn_ctx, x, wo, bo, grad_out, out
                     nc.tensor.transpose(
                         out=turned[:, u, i * P : (i + 1) * P],
                         in_=words[:, i, first + u * P : first + (u + 1) * P],
-                        identity=order[pair][:],
+                        identity=order[:],
                     )
             return turned
 
-        def group(copy, turned, grouped, pair):
-            pairs = grouped[:].bitcast(F32).rearrange("p (r u) -> p r u", u=HALVES)
+        def group(copy, turned, grouped_rows):
             copy(
-                out=pairs[:, pair * BANK_ROWS : (pair + 1) * BANK_ROWS, :],
+                out=grouped_rows.bitcast(F32).rearrange("p (r u) -> p r u", u=HALVES),
                 in_=turned[:].rearrange("p u r -> p r u"),
             )
 
-        g_quantised = {}
+        wo_grouped = {}
         wo_quantised = {}
+        g_quantised = {}
 
-        def prepare(name, loaded, order, x4, quantised, first_pass):
-            passes = range(first_pass, first_pass + LOAD_PASSES)
+        def prepare_wo(s, pair):
+            passes = range(s * LOAD_PASSES, (s + 1) * LOAD_PASSES)
+            for c in passes:
+                if pair == 0:
+                    wo_grouped[c] = wo_stage.tile([P, ROWS * 4], BF16, align_bytes=64, name="wo_grouped")
+                turned = turn(wo_loaded[s][pair], ident, c)
+                group(nc.scalar.copy, turned, wo_grouped[c][:, pair * BANK_ROWS * 4 : (pair + 1) * BANK_ROWS * 4])
+            if pair == PAIRS - 1:
+                for c in passes:
+                    codes = wo_operands.tile([P, ROWS], U32, align_bytes=64, name="wo_codes")
+                    scales = wo_operands.tile([P, ROWS], U8, align_bytes=64, name="wo_scales")
+                    nc.vector.quantize_mx(out=codes[:].bitcast(E4M3_X4), scales=scales[:], in_=wo_grouped[c][:])
+                    wo_quantised[c] = (codes, scales)
+
+        def prepare_g(s, pair):
+            passes = range(s * LOAD_PASSES, (s + 1) * LOAD_PASSES)
             grouped = {}
             for c in passes:
-                grouped[c] = stage.tile([P, ROWS * 4], BF16, align_bytes=64, name="grouped")
-            for pair in range(PAIRS):
-                for c in passes:
-                    copy = nc.vector.tensor_copy if (pair == 0 and c == first_pass) else nc.scalar.copy
-                    group(copy, turn(loaded, order, c, pair), grouped[c], pair)
-                    if pair == PAIRS - 1:
-                        codes = operands.tile([P, ROWS], U32, align_bytes=64, name=name + "_codes")
-                        scales = operands.tile([P, ROWS], U8, align_bytes=64, name=name + "_scales")
-                        nc.vector.quantize_mx(out=codes[:].bitcast(x4), scales=scales[:], in_=grouped[c][:])
-                        quantised[c] = (codes, scales)
+                grouped[c] = g_stage.tile([P, BANK_ROWS * 4], BF16, align_bytes=64, name="g_grouped")
+                turned = turn(g_loaded[s][pair], g_order[pair], c)
+                group(nc.scalar.copy if c == passes[0] else nc.vector.tensor_copy, turned, grouped[c][:])
+            for c in passes:
+                codes = g_operands.tile([P, BANK_ROWS], U32, align_bytes=64, name="g_codes")
+                scales = g_operands.tile([P, BANK_ROWS], U8, align_bytes=64, name="g_scales")
+                nc.vector.quantize_mx(out=codes[:].bitcast(E5M2_X4), scales=scales[:], in_=grouped[c][:])
+                g_quantised[c, pair] = (codes, scales)
 
-        def multiply(c):
-            g_codes, g_scales = g_quantised[c]
-            wo_codes, wo_scales = wo_quantised[c]
-            for m in range(ROW_TILES):
-                b, gi = divmod(m, 2)
-                g_cols = slice((2 * gi + b) * P, (2 * gi + b + 1) * P)
-                nc.tensor.matmul_mx(
-                    out=acc[m][:],
-                    lhsT=g_codes[:, g_cols].bitcast(E5M2_X4),
-                    lhsT_scale=g_scales[:, g_cols],
-                    rhs=wo_codes[:].bitcast(E4M3_X4),
-                    rhs_scale=wo_scales[:],
-                    start=(c == 0),
-                    stop=(c == PASSES - 1),
-                )
+        def multiply(s, pair):
+            for b in range(BANK_TILES):
+                m = 2 * b + pair
+                for c in range(s * LOAD_PASSES, (s + 1) * LOAD_PASSES):
+                    g_codes, g_scales = g_quantised[c, pair]
+                    wo_codes, wo_scales = wo_quantised[c]
+                    nc.tensor.matmul_mx(
+                        out=acc[m][:],
+                        lhsT=g_codes[:, b * P : (b + 1) * P].bitcast(E5M2_X4),
+                        lhsT_scale=g_scales[:, b * P : (b + 1) * P],
+                        rhs=wo_codes[:].bitcast(E4M3_X4),
+                        rhs_scale=wo_scales[:],
+                        start=(c == 0),
+                        stop=(c == PASSES - 1),
+                    )
+                if s == LOADS - 1:
+                    result = results.tile([P, ROWS], F32)
+                    copy = nc.scalar.copy if b == 0 else nc.vector.tensor_copy
+                    copy(out=result[:], in_=acc[m][:])
+                    nc.sync.dma_start(out=out_rows[m * P : (m + 1) * P, :], in_=result[:])
 
-        for k in range(PASSES + LAG):
-            if k < PASSES:
-                first_pass = k // 2 * LOAD_PASSES
-                if k % 2 == 0:
-                    prepare("g", g_loaded, g_order, E5M2_X4, g_quantised, first_pass)
-                else:
-                    prepare("wo", wo_loaded, wo_order, E4M3_X4, wo_quantised, first_pass)
-            if k >= LAG:
-                multiply(k - LAG)
-
-        for m in range(ROW_TILES):
-            result = results.tile([P, ROWS], F32)
-            copy = nc.scalar.copy if m % 2 == 0 else nc.vector.tensor_copy
-            copy(out=result[:], in_=acc[m][:])
-            nc.sync.dma_start(out=out_rows[m * P : (m + 1) * P, :], in_=result[:])
+        quads_after = {}
+        for q in range(QUADS):
+            quads_after.setdefault(min(2 * q + 5, CHUNKS - 1), []).append(q)
+        for j in range(CHUNKS):
+            s, i = divmod(j, 2 * PAIRS)
+            if i < PAIRS:
+                prepare_wo(s, i)
+            else:
+                prepare_g(s, i - PAIRS)
+            for q in quads_after.get(j, []):
+                multiply(q // PAIRS, q % PAIRS)

@@ -109,6 +109,9 @@ def tile_windowattentionblock_pb_k_kernel(tc, attn_ctx, x, wo, bo, grad_out, out
                 in_=turned[:].rearrange("p u r -> p r u"),
             )
 
+        def emptier(pair, c):
+            return nc.vector.tensor_copy if (pair == 0 and c % LOAD_PASSES == 1) else nc.scalar.copy
+
         wo_grouped = {}
         wo_quantised = {}
         g_quantised = {}
@@ -119,7 +122,7 @@ def tile_windowattentionblock_pb_k_kernel(tc, attn_ctx, x, wo, bo, grad_out, out
                 if pair == 0:
                     wo_grouped[c] = wo_stage.tile([P, ROWS * 4], BF16, align_bytes=64, name="wo_grouped")
                 turned = turn(wo_loaded[s][pair], ident, c)
-                group(nc.scalar.copy, turned, wo_grouped[c][:, pair * BANK_ROWS * 4 : (pair + 1) * BANK_ROWS * 4])
+                group(emptier(pair, c), turned, wo_grouped[c][:, pair * BANK_ROWS * 4 : (pair + 1) * BANK_ROWS * 4])
             if pair == PAIRS - 1:
                 for c in passes:
                     codes = wo_operands.tile([P, ROWS], U32, align_bytes=64, name="wo_codes")
@@ -133,7 +136,7 @@ def tile_windowattentionblock_pb_k_kernel(tc, attn_ctx, x, wo, bo, grad_out, out
             for c in passes:
                 grouped[c] = g_stage.tile([P, BANK_ROWS * 4], BF16, align_bytes=64, name="g_grouped")
                 turned = turn(g_loaded[s][pair], g_order[pair], c)
-                group(nc.scalar.copy if c == passes[0] else nc.vector.tensor_copy, turned, grouped[c][:])
+                group(emptier(pair, c), turned, grouped[c][:])
             for c in passes:
                 codes = g_operands.tile([P, BANK_ROWS], U32, align_bytes=64, name="g_codes")
                 scales = g_operands.tile([P, BANK_ROWS], U8, align_bytes=64, name="g_scales")

from contextlib import ExitStack

import concourse.mybir as mybir
from concourse.masks import make_identity

F32 = mybir.dt.float32
BF16 = mybir.dt.bfloat16
U32 = mybir.dt.uint32
U8 = mybir.dt.uint8
E5M2_X4 = mybir.dt.float8_e5m2_x4
E4M3_X4 = mybir.dt.float8_e4m3fn_x4

P = 128
CHANNELS = 8192
ROWS = 512
ROW_TILES = ROWS // P
K_PASS = 512
PASSES = CHANNELS // K_PASS
WORDS_PASS = K_PASS // 2
HALVES = WORDS_PASS // P
BANK_TILES = 2
BANK_ROWS = BANK_TILES * P
PAIRS = ROW_TILES // BANK_TILES
LOAD_PASSES = 2
LOADS = PASSES // LOAD_PASSES
LOAD_K = LOAD_PASSES * K_PASS
CHUNKS = LOADS * 2 * PAIRS
QUADS = LOADS * PAIRS

FLOPS = 2 * ROWS * ROWS * CHANNELS
BYTES = 2 * ROWS * CHANNELS * 2 + ROWS * ROWS * 4


def window_columns(nc, matrix, ident):
    nc.vector.tensor_copy(out=matrix[:, 0, :, :], in_=ident[:, :, 4:12])
    nc.vector.tensor_copy(out=matrix[:, 1, :, 0:4], in_=ident[:, :, 12:16])
    nc.vector.tensor_copy(out=matrix[:, 1, :, 4:8], in_=ident[:, :, 0:4])


def tile_windowattentionblock_pb_k_kernel(tc, attn_ctx, x, wo, bo, grad_out, out):
    nc = tc.nc
    pixels = grad_out.rearrange("b i j c -> b (i j) c")
    wo_rows = wo.rearrange("h d c -> (h d) c").rearrange("(t p) c -> p t c", p=P)
    out_rows = out.rearrange("n t h d -> (n t) (h d)")

    with ExitStack() as ctx:
        ctx.enter_context(tc.manual_schedule())
        consts = ctx.enter_context(tc.tile_pool(name="consts", bufs=1))
        raw = ctx.enter_context(tc.tile_pool(name="raw", bufs=LOADS))
        wo_stage = ctx.enter_context(tc.tile_pool(name="wo_stage", bufs=4))
        g_stage = ctx.enter_context(tc.tile_pool(name="g_stage", bufs=6))
        wo_operands = ctx.enter_context(tc.tile_pool(name="wo_operands", bufs=6))
        g_operands = ctx.enter_context(tc.tile_pool(name="g_operands", bufs=12))
        results = ctx.enter_context(tc.tile_pool(name="results", bufs=ROW_TILES))
        turn_psum = ctx.enter_context(tc.psum_pool(name="turn_psum", bufs=4))
        acc_psum = ctx.enter_context(tc.psum_pool(name="acc_psum", bufs=1))

        g_loaded = []
        wo_loaded = []
        for s in range(LOADS):
            k_cols = slice(s * LOAD_K, (s + 1) * LOAD_K)
            wo_raw0 = raw.tile([P, BANK_TILES, LOAD_K], BF16)
            nc.sync.dma_start(out=wo_raw0[:], in_=wo_rows[:, 0:BANK_TILES, k_cols])
            wo_raw1 = raw.tile([P, BANK_TILES, LOAD_K], BF16)
            nc.sync.dma_start(out=wo_raw1[:], in_=wo_rows[:, BANK_TILES:ROW_TILES, k_cols])
            g_raw0 = raw.tile([P, BANK_TILES, LOAD_K], BF16)
            nc.sync.dma_start(out=g_raw0[:], in_=pixels[:, 64:192, k_cols].rearrange("b p k -> p b k"))
            g_raw1 = raw.tile([P, BANK_TILES, LOAD_K], BF16)
            nc.sync.dma_start(out=g_raw1[0:P:2], in_=pixels[:, 192:256, k_cols].rearrange("b p k -> p b k"))
            nc.sync.dma_start(out=g_raw1[1:P:2], in_=pixels[:, 0:64, k_cols].rearrange("b p k -> p b k"))
            g_loaded.append([g_raw0, g_raw1])
            wo_loaded.append([wo_raw0, wo_raw1])

        ident = consts.tile([P, P], F32)
        make_identity(nc, ident[:])
        order_gi0 = consts.tile([P, P], F32)
        window_columns(
            nc,
            order_gi0[:].rearrange("p (gj ti tj) -> p gj ti tj", gj=2, ti=8),
            ident[:].rearrange("p (ti j) -> p ti j", j=16),
        )
        order_gi1 = consts.tile([P, P], F32)
        for th in range(2):
            window_columns(
                nc,
                order_gi1[:].rearrange("p (gj th i4 tj) -> p gj th i4 tj", gj=2, th=2, i4=4)[:, :, th],
                ident[:].rearrange("p (i4 j th) -> p th i4 j", j=16, th=2)[:, th],
            )
        g_order = [order_gi0, order_gi1]

        acc = [acc_psum.tile([P, ROWS], F32, name="acc%d" % m) for m in range(ROW_TILES)]

        def turn(raw_tile, order, c):
            words = raw_tile[:].bitcast(F32)
            first = (c % LOAD_PASSES) * WORDS_PASS
            turned = turn_psum.tile([P, HALVES, BANK_ROWS], F32)
            for i in range(BANK_TILES):
                for u in range(HALVES):
                    nc.tensor.transpose(
                        out=turned[:, u, i * P : (i + 1) * P],
                        in_=words[:, i, first + u * P : first + (u + 1) * P],
                        identity=order[:],
                    )
            return turned

        def group(copy, turned, grouped_rows):
            copy(
                out=grouped_rows.bitcast(F32).rearrange("p (r u) -> p r u", u=HALVES),
                in_=turned[:].rearrange("p u r -> p r u"),
            )

        def emptier(pair, c):
            return nc.vector.tensor_copy if (pair == 0 and c % LOAD_PASSES == 1) else nc.scalar.copy

        wo_grouped = {}
        wo_quantised = {}
        g_quantised = {}

        def prepare_wo(s, pair):
            passes = range(s * LOAD_PASSES, (s + 1) * LOAD_PASSES)
            for c in passes:
                if pair == 0:
                    wo_grouped[c] = wo_stage.tile([P, ROWS * 4], BF16, align_bytes=64, name="wo_grouped")
                turned = turn(wo_loaded[s][pair], ident, c)
                group(emptier(pair, c), turned, wo_grouped[c][:, pair * BANK_ROWS * 4 : (pair + 1) * BANK_ROWS * 4])
            if pair == PAIRS - 1:
                for c in passes:
                    codes = wo_operands.tile([P, ROWS], U32, align_bytes=64, name="wo_codes")
                    scales = wo_operands.tile([P, ROWS], U8, align_bytes=64, name="wo_scales")
                    nc.vector.quantize_mx(out=codes[:].bitcast(E4M3_X4), scales=scales[:], in_=wo_grouped[c][:])
                    wo_quantised[c] = (codes, scales)

        def prepare_g(s, pair):
            passes = range(s * LOAD_PASSES, (s + 1) * LOAD_PASSES)
            grouped = {}
            for c in passes:
                grouped[c] = g_stage.tile([P, BANK_ROWS * 4], BF16, align_bytes=64, name="g_grouped")
                turned = turn(g_loaded[s][pair], g_order[pair], c)
                group(emptier(pair, c), turned, grouped[c][:])
            for c in passes:
                codes = g_operands.tile([P, BANK_ROWS], U32, align_bytes=64, name="g_codes")
                scales = g_operands.tile([P, BANK_ROWS], U8, align_bytes=64, name="g_scales")
                nc.vector.quantize_mx(out=codes[:].bitcast(E5M2_X4), scales=scales[:], in_=grouped[c][:])
                g_quantised[c, pair] = (codes, scales)

        def multiply(s, pair):
            for b in range(BANK_TILES):
                m = 2 * b + pair
                for c in range(s * LOAD_PASSES, (s + 1) * LOAD_PASSES):
                    g_codes, g_scales = g_quantised[c, pair]
                    wo_codes, wo_scales = wo_quantised[c]
                    nc.tensor.matmul_mx(
                        out=acc[m][:],
                        lhsT=g_codes[:, b * P : (b + 1) * P].bitcast(E5M2_X4),
                        lhsT_scale=g_scales[:, b * P : (b + 1) * P],
                        rhs=wo_codes[:].bitcast(E4M3_X4),
                        rhs_scale=wo_scales[:],
                        start=(c == 0),
                        stop=(c == PASSES - 1),
                    )
                if s == LOADS - 1:
                    result = results.tile([P, ROWS], F32)
                    copy = nc.scalar.copy if b == 0 else nc.vector.tensor_copy
                    copy(out=result[:], in_=acc[m][:])
                    nc.sync.dma_start(out=out_rows[m * P : (m + 1) * P, :], in_=result[:])

        quads_after = {}
        for q in range(QUADS):
            quads_after.setdefault(min(2 * q + 5, CHUNKS - 1), []).append(q)
        for j in range(CHUNKS):
            s, i = divmod(j, 2 * PAIRS)
            if i < PAIRS:
                prepare_wo(s, i)
            else:
                prepare_g(s, i - PAIRS)
            for q in quads_after.get(j, []):
                multiply(q // PAIRS, q % PAIRS)
